import numpy as np
import ml_dtypes


def mxq(x, axis, fmt="e4m3"):
    dtype, down = {"e4m3": (ml_dtypes.float8_e4m3fn, 7), "e5m2": (ml_dtypes.float8_e5m2, 14)}[fmt]
    v = np.moveaxis(np.asarray(x, np.float32).astype(ml_dtypes.bfloat16).astype(np.float64), axis, -1)
    blocks = v.reshape(v.shape[:-1] + (-1, 32))
    amax = np.abs(blocks).max(-1, keepdims=True)
    byte = np.maximum(np.where(amax > 0, np.frexp(amax)[1] - 1 + 127, 0) - down, 1)
    scale = np.exp2(byte - 127.0)
    codes = (blocks / scale).astype(np.float32).astype(dtype).astype(np.float64)
    return np.moveaxis((codes * scale).reshape(v.shape), -1, axis)


WIDE = False


def mx_kscale(k):
    if not WIDE:
        return np.ones(k)
    levels = np.array([10, -10, 5, -5, 0])
    if k % 512:
        return np.exp2(np.random.permutation(np.resize(levels, k // 32))).repeat(32)
    a = np.empty((k // 512, 16))
    for p in range(k // 512):
        a[p, :8] = np.random.permutation(np.resize(levels, 8))
        for g in range(8):
            far = levels[np.abs(levels - a[p, g]) >= 10]
            a[p, g + 8] = far[np.random.randint(len(far))]
    return np.exp2(a.ravel()).repeat(32)


BF16 = ml_dtypes.bfloat16


def bf(x):
    return np.asarray(x, np.float32).astype(BF16)


def f64(x):
    return np.asarray(x).astype(np.float64)


B, K, NH, N = 512, 2048, 4096, 1024
EPSILON = 0.1


def setup_inputs():
    s = mx_kscale(K)
    g = 1.0 / np.mean(1.0 / s)
    return {"x": bf(np.random.standard_normal((B, K)) * s),
            "y": bf(np.random.standard_normal((B, N)) * 12.0 / np.sqrt(K) * g),
            "beta": bf(np.random.random((K, N)) * 1.7 / np.sqrt(K) / s[:, None]),
            "bias_lin": bf(np.random.standard_normal(N) * 0.1),
            "W1": bf(-np.random.random((NH, K)) * 1.7 / np.sqrt(K) / s[None, :]),
            "W2": bf(np.random.random((N, NH)) * (0.5 + np.random.random((N, 1))) * 2.0 / NH**2),
            "bias1": bf(np.random.standard_normal(NH) * 0.1),
            "bias2": bf(np.random.standard_normal(N) * 0.1),
            "adv": 1}


def reference(x, y, beta, bias_lin, W1, W2, bias1, bias2, adv):
    xq = mxq(f64(x), 1, "e4m3")
    lin = (xq @ mxq(f64(beta), 0, "e4m3")) + f64(bias_lin)
    if adv:
        beta_norm = np.sum(np.abs(f64(beta)), axis=0)
        lin = lin - EPSILON * f64(y) * beta_norm
    if adv:
        one = NH * np.sum(f64(W2), axis=1) + f64(bias2)
        one = np.broadcast_to(one, lin.shape)
    else:
        h = np.maximum((xq @ mxq(f64(W1), 1, "e4m3").T) + f64(bias1), 0.0)
        one = (mxq(h, 1, "e4m3") @ mxq(f64(W2), 1, "e4m3").T) + f64(bias2)
    return lin + one

@@ -1,0 +1,335 @@
+from contextlib import ExitStack
+
+import concourse.mybir as mybir
+from concourse.masks import make_identity
+
+F32 = mybir.dt.float32
+BF16 = mybir.dt.bfloat16
+I32 = mybir.dt.int32
+U32 = mybir.dt.uint32
+U8 = mybir.dt.uint8
+FP8X4 = mybir.dt.float8_e4m3fn_x4
+ALU = mybir.AluOpType
+ACT = mybir.ActivationFunctionType
+
+P = 128
+B, K, NH, N = 512, 2048, 4096, 1024
+EPSILON = 0.1
+K_PASS = 4 * P
+PASSES = K // K_PASS
+PASS_ELEMS = 4 * N
+HALF = N // 2
+JT = N // P
+BT = B // P
+W2_HALF = NH // 2
+ONES_N = 32
+
+FLOPS = 2 * B * K * N
+BYTES = 2 * (B * K + B * N + K * N + N * NH + 2 * N) + 4 * B * N
+
+W2_LOAD_ORDER = (0, 1, 3, 2, 6, 4, 5)
+SPLIT_TILES = (3, 6, 7)
+
+
+def tile_advresnet_kernel(tc, x, y, beta, bias_lin, W1, W2, bias1, bias2, adv, out):
+    assert adv == 1
+    nc = tc.nc
+    with ExitStack() as ctx:
+        const = ctx.enter_context(tc.tile_pool(name="const", bufs=1))
+        big = ctx.enter_context(tc.tile_pool(name="big", bufs=1))
+        work = ctx.enter_context(tc.tile_pool(name="work", bufs=2))
+        ps_a = ctx.enter_context(tc.psum_pool(name="ps_a", bufs=3))
+        ps_b = ctx.enter_context(tc.psum_pool(name="ps_b", bufs=3))
+        ps_c = ctx.enter_context(tc.psum_pool(name="ps_c", bufs=2))
+        ctx.enter_context(tc.manual_schedule())
+
+        brows = const.tile([P, P], BF16, name="brows")
+        nc.gpsimd.memset(brows[:], 0.0)
+        nc.scalar.dma_start(out=brows[0:JT, :], in_=bias_lin.rearrange("(r c) -> r c", c=P))
+        nc.scalar.dma_start(out=brows[JT : 2 * JT, :], in_=bias2.rearrange("(r c) -> r c", c=P))
+        ident_b = const.tile([P, P], BF16, name="ident_b")
+        make_identity(nc, ident_b[:])
+        ident_f = const.tile([P, P], F32, name="ident_f")
+        make_identity(nc, ident_f[:])
+        ones = const.tile([P, ONES_N], BF16, name="ones")
+        nc.vector.memset(ones[:], 1.0)
+
+        raw = big.tile([P, PASSES * PASS_ELEMS], BF16, name="raw", tag="raw_tt")
+        raw_planes = raw[:].rearrange("q (g t w) -> q g t w", g=PASSES, t=4)
+        for h in range(2):
+            for u in range(2):
+                nc.sync.dma_start(
+                    out=raw_planes[:, 0, 2 * u : 2 * u + 2, HALF * h : HALF * (h + 1)],
+                    in_=beta[0:K_PASS, HALF * h : HALF * (h + 1)].rearrange("(q t) w -> q t w", t=4)[
+                        :, 2 * u : 2 * u + 2, :
+                    ],
+                )
+        for g in range(1, PASSES):
+            nc.sync.dma_start(
+                out=raw[:, PASS_ELEMS * g : PASS_ELEMS * (g + 1)],
+                in_=beta[K_PASS * g : K_PASS * (g + 1), :].rearrange("(q t) w -> q (t w)", t=4),
+            )
+        x_sb = big.tile([P, BT * K], BF16, name="x_sb", tag="x_out")
+        x_rows = x.rearrange("(p t) k -> p (t k)", t=BT)
+        for h in range(2):
+            nc.sync.dma_start(out=x_sb[:, 2 * K * h : 2 * K * (h + 1)], in_=x_rows[:, 2 * K * h : 2 * K * (h + 1)])
+        y_sb = big.tile([P, BT * N], BF16, name="y_sb")
+        nc.sync.dma_start(out=y_sb[:], in_=y.rearrange("(p t) j -> p (t j)", t=BT))
+        w2 = [big.tile([P, NH], BF16, name="w2_%d" % jt) for jt in range(JT)]
+        for jt in W2_LOAD_ORDER:
+            nc.sync.dma_start(out=w2[jt][:], in_=W2[P * jt : P * (jt + 1), :])
+        for i in range(2):
+            nc.sync.dma_start(
+                out=w2[JT - 1][:, W2_HALF * i : W2_HALF * (i + 1)],
+                in_=W2[P * (JT - 1) : P * JT, W2_HALF * i : W2_HALF * (i + 1)],
+            )
+
+        codes_b = big.tile([P, PASSES * N], U32, name="codes_b", align_bytes=64)
+        scales_b = big.tile([P, PASSES * N], U8, name="plane_b", align_bytes=64)
+        codes_x = big.tile([P, PASSES * B], U32, name="codes_x", align_bytes=64)
+        scales_x = big.tile([P, PASSES * B], U8, name="plane_x", align_bytes=64)
+        b16 = const.tile([P, 2 * JT], F32, name="b16")
+        bsum = const.tile([P, JT], F32, name="bsum")
+        norm = const.tile([P, JT], F32, name="sraw")
+        y_scale = const.tile([P, JT], F32, name="s_col")
+        w2_sum = [const.tile([P, 1], F32, name="c_%d" % jt) for jt in range(JT)]
+        half_a = dict((jt, const.tile([P, 1], F32, name="pa_%d" % jt)) for jt in SPLIT_TILES)
+        half_b = dict((jt, const.tile([P, 1], F32, name="pb_%d" % jt)) for jt in SPLIT_TILES)
+        x_words = x_sb[:].bitcast(F32)
+        out_rows = out.rearrange("(p t) j -> p t j", t=BT)
+        held = {}
+
+        bias_t = ps_c.tile([P, P], BF16, name="bt_ps", tag="c")
+        nc.tensor.transpose(out=bias_t[:], in_=brows[:], identity=ident_b[:])
+        norm_ps = [ps_b.tile([P, JT // 2, PASSES, ONES_N], F32, name="bn_%d" % i, tag="b") for i in range(2)]
+
+        def bias_columns():
+            nc.vector.tensor_copy(out=b16[:], in_=bias_t[:, 0 : 2 * JT])
+            nc.vector.tensor_tensor(out=bsum[:], in0=b16[:, 0:JT], in1=b16[:, JT : 2 * JT], op=ALU.add)
+
+        def beta_abs(g):
+            ab = work.tile([P, PASS_ELEMS // 2], I32, name="ab", tag="ab")
+            nc.vector.tensor_single_scalar(
+                out=ab[:],
+                in_=raw[:, PASS_ELEMS * g : PASS_ELEMS * (g + 1)].bitcast(I32),
+                scalar=0x7FFF7FFF,
+                op=ALU.bitwise_and,
+            )
+            held["ab", g] = ab
+
+        def beta_regroup(g, h, on_vector):
+            grouped = work.tile([P, 4 * HALF], BF16, name="gb", tag="gb", bufs=2 * PASSES, align_bytes=64)
+            src = raw_planes[:, g, :, HALF * h : HALF * (h + 1)].rearrange("q t (c i) -> q c t i", i=4)
+            dst = grouped[:].rearrange("q (c i t) -> q c t i", i=4, t=4)
+            if on_vector:
+                nc.vector.tensor_copy(out=dst, in_=src)
+            else:
+                nc.scalar.copy(out=dst, in_=src)
+            held["gb", g, h] = grouped
+
+        def beta_quantise(g, h):
+            cols = slice(N * g + HALF * h, N * g + HALF * (h + 1))
+            nc.vector.quantize_mx(
+                out=codes_b[:, cols].bitcast(FP8X4), scales=scales_b[:, cols], in_=held["gb", g, h][:]
+            )
+
+        def beta_norm_pass(g):
+            planes = held["ab", g][:].bitcast(BF16)
+            for jt in range(JT):
+                for t in range(4):
+                    nc.tensor.matmul(
+                        out=norm_ps[jt // 4][:, jt % 4, g, :],
+                        lhsT=planes[:, N * t + P * jt : N * t + P * (jt + 1)],
+                        rhs=ones[:],
+                        start=(t == 0),
+                        stop=(t == 3),
+                    )
+
+        def norm_columns():
+            for i in range(2):
+                nc.vector.tensor_reduce(
+                    out=norm[:, 4 * i : 4 * (i + 1)], in_=norm_ps[i][:, :, :, 0], axis=mybir.AxisListType.X, op=ALU.add
+                )
+            nc.vector.tensor_scalar_mul(out=y_scale[:], in0=norm[:], scalar1=-EPSILON)
+
+        def x_turn(i):
+            h, g = i // PASSES, i % PASSES
+            turned = ps_a.tile([P, 2, 2 * P], F32, name="xt", tag="a")
+            for u in range(2):
+                for s in range(2):
+                    w0 = (K // 2) * (2 * h + s) + 256 * g
+                    nc.tensor.transpose(
+                        out=turned[:, u, P * s : P * (s + 1)],
+                        in_=x_words[:, w0 + u : w0 + 256 : 2],
+                        identity=ident_f[:],
+                    )
+            grouped = work.tile([P, 8 * P], BF16, name="gx", tag="gx", bufs=2 * PASSES, align_bytes=64)
+            nc.scalar.copy(
+                out=grouped[:].bitcast(F32).rearrange("q (c u) -> q c u", u=2),
+                in_=turned[:].rearrange("q u c -> q c u"),
+            )
+            held["gx", i] = grouped
+
+        def x_quantise(i):
+            h, g = i // PASSES, i % PASSES
+            cols = slice(B * g + 2 * P * h, B * g + 2 * P * (h + 1))
+            nc.vector.quantize_mx(out=codes_x[:, cols].bitcast(FP8X4), scales=scales_x[:, cols], in_=held["gx", i][:])
+
+        def y_turn(m):
+            turned = ps_c.tile([P, 2, B], BF16, name="y_t", tag="c")
+            for i in range(2):
+                jt = 2 * m + i
+                for t in range(BT):
+                    nc.tensor.transpose(
+                        out=turned[:, i, P * t : P * (t + 1)],
+                        in_=y_sb[:, N * t + P * jt : N * t + P * (jt + 1)],
+                        identity=ident_b[:],
+                    )
+            held["y_t", m] = turned
+
+        def y_term(jt):
+            nc.scalar.activation(
+                out=held["y_terms"][:, jt, :],
+                in_=held["y_t", jt // 2][:, jt % 2, :],
+                func=ACT.Identity,
+                scale=y_scale[:, jt : jt + 1],
+                bias=bsum[:, jt : jt + 1],
+            )
+
+        def product(jt):
+            acc = ps_a.tile([P, B], F32, name="mm", tag="a")
+            for g in range(PASSES):
+                j_cols = slice(N * g + P * jt, N * g + P * (jt + 1))
+                b_cols = slice(B * g, B * (g + 1))
+                nc.tensor.matmul_mx(
+                    out=acc[:],
+                    lhsT=codes_b[:, j_cols].bitcast(FP8X4),
+                    lhsT_scale=scales_b[:, j_cols],
+                    rhs=codes_x[:, b_cols].bitcast(FP8X4),
+                    rhs_scale=scales_x[:, b_cols],
+                    start=(g == 0),
+                    stop=(g == PASSES - 1),
+                )
+            held["mm", jt] = acc
+
+        def sum_on_vector(piece, total):
+            nc.vector.tensor_scalar(
+                out=piece, in0=piece, scalar1=float(NH), scalar2=None, op0=ALU.mult, op1=ALU.add, accum_out=total
+            )
+
+        def sum_on_scalar(piece, total):
+            nc.scalar.activation(out=piece, in_=piece, func=ACT.Copy, scale=float(NH), accum_out=total)
+
+        def join_halves(jt):
+            nc.vector.tensor_tensor(out=w2_sum[jt][:], in0=half_a[jt][:], in1=half_b[jt][:], op=ALU.add)
+
+        def combine(jt):
+            tile_t = work.tile([P, B], F32, name="o_t", tag="o_t", bufs=3)
+            nc.vector.scalar_tensor_tensor(
+                out=tile_t[:],
+                in0=held["mm", jt][:],
+                scalar=w2_sum[jt][:, 0:1],
+                in1=held["y_terms"][:, jt, :],
+                op0=ALU.add,
+                op1=ALU.add,
+            )
+            turned = ps_b.tile([P, BT, P], F32, name="o_ps", tag="b")
+            for t in range(BT):
+                nc.tensor.transpose(out=turned[:, t, :], in_=tile_t[:, P * t : P * (t + 1)], identity=ident_f[:])
+            held["o_ps", jt] = turned
+
+        def leave_psum(jt):
+            nc.scalar.copy(out=held["out_sb"][:, :, P * jt : P * (jt + 1)], in_=held["o_ps", jt][:])
+
+        def store(first, end):
+            cols = slice(P * first, P * end)
+            nc.sync.dma_start(out=out_rows[:, :, cols], in_=held["out_sb"][:, :, cols])
+
+        left, right = slice(0, W2_HALF), slice(W2_HALF, NH)
+
+        beta_regroup(0, 0, True)
+        beta_regroup(0, 1, False)
+        beta_abs(0)
+        beta_quantise(0, 0)
+        bias_columns()
+        beta_norm_pass(0)
+        beta_abs(1)
+        beta_regroup(1, 0, True)
+        beta_regroup(1, 1, False)
+        beta_quantise(0, 1)
+        beta_quantise(1, 0)
+        beta_norm_pass(1)
+        beta_abs(2)
+        beta_norm_pass(2)
+        beta_abs(3)
+        beta_norm_pass(3)
+        beta_regroup(2, 0, True)
+        beta_regroup(2, 1, False)
+        beta_quantise(1, 1)
+        beta_quantise(2, 0)
+        beta_regroup(3, 1, False)
+        beta_regroup(3, 0, True)
+        beta_quantise(2, 1)
+        norm_columns()
+
+        for i in range(2 * PASSES):
+            x_turn(i)
+        beta_quantise(3, 1)
+        beta_quantise(3, 0)
+        for i in range(2 * PASSES):
+            x_quantise(i)
+
+        held["y_terms"] = big.tile([P, JT, B], F32, name="t_all", tag="raw_tt")
+        y_turn(0)
+        y_turn(1)
+        for jt in range(4):
+            y_term(jt)
+        y_turn(2)
+        product(0)
+        y_turn(3)
+        for jt in range(4, JT):
+            y_term(jt)
+        product(1)
+        product(2)
+
+        held["out_sb"] = big.tile([P, BT, N], F32, name="out_sb", tag="x_out")
+        sum_on_vector(w2[0][:], w2_sum[0][:])
+        sum_on_vector(w2[1][:], w2_sum[1][:])
+        sum_on_scalar(w2[3][:, left], half_a[3][:])
+        sum_on_scalar(w2[3][:, right], half_b[3][:])
+        combine(0)
+        product(3)
+        leave_psum(0)
+        combine(1)
+        product(4)
+        leave_psum(1)
+        store(0, 2)
+        sum_on_vector(w2[2][:], w2_sum[2][:])
+        sum_on_scalar(w2[6][:, left], half_a[6][:])
+        combine(2)
+        product(5)
+        join_halves(3)
+        combine(3)
+        product(6)
+        leave_psum(2)
+        leave_psum(3)
+        store(2, 4)
+        sum_on_scalar(w2[6][:, right], half_b[6][:])
+        sum_on_vector(w2[4][:], w2_sum[4][:])
+        combine(4)
+        product(7)
+        sum_on_vector(w2[5][:], w2_sum[5][:])
+        leave_psum(4)
+        sum_on_scalar(w2[7][:, left], half_a[7][:])
+        combine(5)
+        join_halves(6)
+        combine(6)
+        leave_psum(5)
+        store(4, 6)
+        leave_psum(6)
+        store(6, 7)
+        sum_on_vector(w2[7][:, right], half_b[7][:])
+        join_halves(7)
+        combine(7)
+        leave_psum(7)
+        store(7, 8)

@@ -22,13 +22,16 @@ HALF = N // 2
 JT = N // P
 BT = B // P
 W2_HALF = NH // 2
-ONES_N = 32
+ONES_N = 16
 
 FLOPS = 2 * B * K * N
 BYTES = 2 * (B * K + B * N + K * N + N * NH + 2 * N) + 4 * B * N
 
-W2_LOAD_ORDER = (0, 1, 3, 2, 6, 4, 5)
-SPLIT_TILES = (3, 6, 7)
+PE_TILES = (3, 5,)
+SPLIT_TILES = (2, 6, 7,)
+SPREAD = 4
+PE_COLS = NH // SPREAD
+PE_ROWS = P // SPREAD
 
 
 def tile_advresnet_kernel(tc, x, y, beta, bias_lin, W1, W2, bias1, bias2, adv, out):
@@ -45,14 +48,23 @@ def tile_advresnet_kernel(tc, x, y, beta, bias_lin, W1, W2, bias1, bias2, adv, o
 
         brows = const.tile([P, P], BF16, name="brows")
         nc.gpsimd.memset(brows[:], 0.0)
+        ones = const.tile([P, ONES_N], BF16, name="ones")
+        nc.vector.memset(ones[:], 1.0)
+        table_load = const.tile([P, 1], BF16, name="table_load")
+        nc.scalar.copy(out=table_load[:], in_=ones[:, 0:1])
         nc.scalar.dma_start(out=brows[0:JT, :], in_=bias_lin.rearrange("(r c) -> r c", c=P))
         nc.scalar.dma_start(out=brows[JT : 2 * JT, :], in_=bias2.rearrange("(r c) -> r c", c=P))
         ident_b = const.tile([P, P], BF16, name="ident_b")
         make_identity(nc, ident_b[:])
         ident_f = const.tile([P, P], F32, name="ident_f")
         make_identity(nc, ident_f[:])
-        ones = const.tile([P, ONES_N], BF16, name="ones")
-        nc.vector.memset(ones[:], 1.0)
+
+        pairs = const.tile([P, P // 2], BF16, name="pairs")
+        nc.vector.tensor_tensor(out=pairs[:], in0=ident_b[:, 0::2], in1=ident_b[:, 1::2], op=ALU.add)
+        quads = const.tile([P, PE_ROWS], BF16, name="quads")
+        nc.vector.tensor_tensor(out=quads[:], in0=pairs[:, 0::2], in1=pairs[:, 1::2], op=ALU.add)
+        factor = const.tile([P, 1], F32, name="factor")
+        nc.vector.memset(factor[:], float(NH))
 
         raw = big.tile([P, PASSES * PASS_ELEMS], BF16, name="raw", tag="raw_tt")
         raw_planes = raw[:].rearrange("q (g t w) -> q g t w", g=PASSES, t=4)
@@ -64,25 +76,46 @@ def tile_advresnet_kernel(tc, x, y, beta, bias_lin, W1, W2, bias1, bias2, adv, o
                         :, 2 * u : 2 * u + 2, :
                     ],
                 )
-        for g in range(1, PASSES):
+        def load_beta(g):
             nc.sync.dma_start(
                 out=raw[:, PASS_ELEMS * g : PASS_ELEMS * (g + 1)],
                 in_=beta[K_PASS * g : K_PASS * (g + 1), :].rearrange("(q t) w -> q (t w)", t=4),
             )
+
         x_sb = big.tile([P, BT * K], BF16, name="x_sb", tag="x_out")
         x_rows = x.rearrange("(p t) k -> p (t k)", t=BT)
-        for h in range(2):
+
+        def load_x(h):
             nc.sync.dma_start(out=x_sb[:, 2 * K * h : 2 * K * (h + 1)], in_=x_rows[:, 2 * K * h : 2 * K * (h + 1)])
+
         y_sb = big.tile([P, BT * N], BF16, name="y_sb")
-        nc.sync.dma_start(out=y_sb[:], in_=y.rearrange("(p t) j -> p (t j)", t=BT))
         w2 = [big.tile([P, NH], BF16, name="w2_%d" % jt) for jt in range(JT)]
-        for jt in W2_LOAD_ORDER:
-            nc.sync.dma_start(out=w2[jt][:], in_=W2[P * jt : P * (jt + 1), :])
-        for i in range(2):
-            nc.sync.dma_start(
-                out=w2[JT - 1][:, W2_HALF * i : W2_HALF * (i + 1)],
-                in_=W2[P * (JT - 1) : P * JT, W2_HALF * i : W2_HALF * (i + 1)],
-            )
+
+        def load_w2(jt, first, end):
+            rows = W2[P * jt : P * (jt + 1), :]
+            if jt in PE_TILES:
+                nc.sync.dma_start(
+                    out=w2[jt][:].rearrange("p (s w) -> p s w", s=SPREAD),
+                    in_=rows.rearrange("(s r) (c w) -> (r c) s w", s=SPREAD, c=SPREAD),
+                )
+            else:
+                nc.sync.dma_start(out=w2[jt][:, first:end], in_=rows[:, first:end])
+
+        load_beta(1)
+        load_x(0)
+        load_beta(2)
+        load_x(1)
+        load_beta(3)
+        load_w2(0, 0, NH)
+        nc.sync.dma_start(out=y_sb[:], in_=y.rearrange("(p t) j -> p (t j)", t=BT))
+        load_w2(1, 0, NH)
+        load_w2(3, 0, NH)
+        load_w2(2, 0, NH)
+        load_w2(5, 0, NH)
+        load_w2(4, 0, NH)
+        load_w2(6, 0, NH)
+        load_w2(7, 0,2048)
+        load_w2(7, 2048,NH)
 
         codes_b = big.tile([P, PASSES * N], U32, name="codes_b", align_bytes=64)
         scales_b = big.tile([P, PASSES * N], U8, name="plane_b", align_bytes=64)
@@ -92,9 +125,8 @@ def tile_advresnet_kernel(tc, x, y, beta, bias_lin, W1, W2, bias1, bias2, adv, o
         bsum = const.tile([P, JT], F32, name="bsum")
         norm = const.tile([P, JT], F32, name="sraw")
         y_scale = const.tile([P, JT], F32, name="s_col")
-        w2_sum = [const.tile([P, 1], F32, name="c_%d" % jt) for jt in range(JT)]
-        half_a = dict((jt, const.tile([P, 1], F32, name="pa_%d" % jt)) for jt in SPLIT_TILES)
-        half_b = dict((jt, const.tile([P, 1], F32, name="pb_%d" % jt)) for jt in SPLIT_TILES)
+        w2_sum = dict((jt, const.tile([P, 1], F32, name="c_%d" % jt)) for jt in range(JT) if jt not in PE_TILES)
+        part = dict(((jt, i), const.tile([P, 1], F32, name="part_%d_%d" % (jt, i))) for jt in SPLIT_TILES for i in range(2))
         x_words = x_sb[:].bitcast(F32)
         out_rows = out.rearrange("(p t) j -> p t j", t=BT)
         held = {}
@@ -126,6 +158,13 @@ def tile_advresnet_kernel(tc, x, y, beta, bias_lin, W1, W2, bias1, bias2, adv, o
             else:
                 nc.scalar.copy(out=dst, in_=src)
             held["gb", g, h] = grouped
+
+        def beta_regroup_part(g, h, first, end, copy):
+            if ("gb", g, h) not in held:
+                held["gb", g, h] = work.tile([P, 4 * HALF], BF16, name="gb", tag="gb", bufs=2 * PASSES, align_bytes=64)
+            src = raw_planes[:, g, :, HALF * h + first : HALF * h + end].rearrange("q t (c i) -> q c t i", i=4)
+            dst = held["gb", g, h][:, 4 * first : 4 * end].rearrange("q (c i t) -> q c t i", i=4, t=4)
+            copy(out=dst, in_=src)
 
         def beta_quantise(g, h):
             cols = slice(N * g + HALF * h, N * g + HALF * (h + 1))
@@ -196,39 +235,74 @@ def tile_advresnet_kernel(tc, x, y, beta, bias_lin, W1, W2, bias1, bias2, adv, o
                 bias=bsum[:, jt : jt + 1],
             )
 
-        def product(jt):
-            acc = ps_a.tile([P, B], F32, name="mm", tag="a")
-            for g in range(PASSES):
-                j_cols = slice(N * g + P * jt, N * g + P * (jt + 1))
-                b_cols = slice(B * g, B * (g + 1))
-                nc.tensor.matmul_mx(
-                    out=acc[:],
-                    lhsT=codes_b[:, j_cols].bitcast(FP8X4),
-                    lhsT_scale=scales_b[:, j_cols],
-                    rhs=codes_x[:, b_cols].bitcast(FP8X4),
-                    rhs_scale=scales_x[:, b_cols],
-                    start=(g == 0),
-                    stop=(g == PASSES - 1),
-                )
-            held["mm", jt] = acc
-
-        def sum_on_vector(piece, total):
-            nc.vector.tensor_scalar(
-                out=piece, in0=piece, scalar1=float(NH), scalar2=None, op0=ALU.mult, op1=ALU.add, accum_out=total
+        def product_pass(jt, g):
+            if g == 0:
+                held["mm", jt] = ps_a.tile([P, B], F32, name="mm", tag="a")
+            j_cols = slice(N * g + P * jt, N * g + P * (jt + 1))
+            b_cols = slice(B * g, B * (g + 1))
+            nc.tensor.matmul_mx(
+                out=held["mm", jt][:],
+                lhsT=codes_b[:, j_cols].bitcast(FP8X4),
+                lhsT_scale=scales_b[:, j_cols],
+                rhs=codes_x[:, b_cols].bitcast(FP8X4),
+                rhs_scale=scales_x[:, b_cols],
+                start=(g == 0),
+                stop=(g == PASSES - 1),
             )
 
-        def sum_on_scalar(piece, total):
-            nc.scalar.activation(out=piece, in_=piece, func=ACT.Copy, scale=float(NH), accum_out=total)
+        def product(jt):
+            for g in range(PASSES):
+                product_pass(jt, g)
+
+        def sum_on_vector(jt, first, end, total, before=None):
+            piece = w2[jt][:, first:end]
+            nc.vector.tensor_scalar(
+                out=piece,
+                in0=piece,
+                scalar1=float(NH),
+                scalar2=None if before is None else before[:],
+                op0=ALU.mult,
+                op1=ALU.add,
+                accum_out=total[:],
+            )
+
+        def sum_on_scalar(jt, first, end, total):
+            piece = w2[jt][:, first:end]
+            nc.scalar.activation(out=piece, in_=piece, func=ACT.Copy, scale=float(NH), accum_out=total[:])
 
         def join_halves(jt):
-            nc.vector.tensor_tensor(out=w2_sum[jt][:], in0=half_a[jt][:], in1=half_b[jt][:], op=ALU.add)
+            nc.vector.tensor_tensor(out=w2_sum[jt][:], in0=part[jt, 0][:], in1=part[jt, 1][:], op=ALU.add)
+
+        def sum_on_tensor(jt):
+            sums = ps_c.tile([P, P + 1], F32, name="w2_ps", tag="c")
+            for s in range(SPREAD):
+                for i in range(PE_COLS // P):
+                    c0 = PE_COLS * s + P * i
+                    nc.tensor.matmul(
+                        out=sums[:, PE_ROWS * s : PE_ROWS * (s + 1)],
+                        lhsT=w2[jt][:, c0 : c0 + P],
+                        rhs=quads[:],
+                        start=(i == 0),
+                        stop=(i == PE_COLS // P - 1),
+                    )
+            held["w2_ps", jt] = sums
+
+        def gather(jt, copy):
+            held["partial", jt] = work.tile([P, P], F32, name="partial", tag="partial")
+            copy(out=held["partial", jt][:], in_=held["w2_ps", jt][:, 0:P])
+
+        def total_on_tensor(jt):
+            held["total", jt] = held["w2_ps", jt][:, P : P + 1]
+            nc.tensor.matmul(
+                out=held["total", jt], lhsT=held["partial", jt][:], rhs=factor[:], start=True, stop=True
+            )
 
         def combine(jt):
             tile_t = work.tile([P, B], F32, name="o_t", tag="o_t", bufs=3)
             nc.vector.scalar_tensor_tensor(
                 out=tile_t[:],
                 in0=held["mm", jt][:],
-                scalar=w2_sum[jt][:, 0:1],
+                scalar=held["total", jt] if jt in PE_TILES else w2_sum[jt][:],
                 in1=held["y_terms"][:, jt, :],
                 op0=ALU.add,
                 op1=ALU.add,
@@ -238,14 +312,43 @@ def tile_advresnet_kernel(tc, x, y, beta, bias_lin, W1, W2, bias1, bias2, adv, o
                 nc.tensor.transpose(out=turned[:, t, :], in_=tile_t[:, P * t : P * (t + 1)], identity=ident_f[:])
             held["o_ps", jt] = turned
 
+        def combine_halves(jt):
+            tile_t = work.tile([P, B], F32, name="o_t", tag="o_t", bufs=3)
+            turned = [ps_b.tile([P, 2, P], F32, name="o_half%d" % i, tag="b") for i in range(2)]
+            held["o_half", jt] = turned
+            for i in range(2):
+                cols = slice(B // 2 * i, B // 2 * (i + 1))
+                nc.vector.scalar_tensor_tensor(
+                    out=tile_t[:, cols],
+                    in0=held["mm", jt][:, cols],
+                    scalar=held["total", jt] if jt in PE_TILES else w2_sum[jt][:],
+                    in1=held["y_terms"][:, jt, cols],
+                    op0=ALU.add,
+                    op1=ALU.add,
+                )
+            for i in range(2):
+                for t in range(2):
+                    nc.tensor.transpose(
+                        out=turned[i][:, t, :], in_=tile_t[:, P * (2 * i + t) : P * (2 * i + t + 1)], identity=ident_f[:]
+                    )
+
+        def leave_halves(jt):
+            nc.scalar.copy(out=held["out_sb"][:, 0:2, P * jt : P * (jt + 1)], in_=held["o_half", jt][0][:])
+            nc.vector.tensor_copy(out=held["out_sb"][:, 2:4, P * jt : P * (jt + 1)], in_=held["o_half", jt][1][:])
+
+        def store_halves(jt):
+            cols = slice(P * jt, P * (jt + 1))
+            for i in range(2):
+                nc.sync.dma_start(
+                    out=out_rows[:, 2 * i : 2 * (i + 1), cols], in_=held["out_sb"][:, 2 * i : 2 * (i + 1), cols]
+                )
+
         def leave_psum(jt):
             nc.scalar.copy(out=held["out_sb"][:, :, P * jt : P * (jt + 1)], in_=held["o_ps", jt][:])
 
         def store(first, end):
             cols = slice(P * first, P * end)
             nc.sync.dma_start(out=out_rows[:, :, cols], in_=held["out_sb"][:, :, cols])
-
-        left, right = slice(0, W2_HALF), slice(W2_HALF, NH)
 
         beta_regroup(0, 0, True)
         beta_regroup(0, 1, False)
@@ -259,77 +362,94 @@ def tile_advresnet_kernel(tc, x, y, beta, bias_lin, W1, W2, bias1, bias2, adv, o
         beta_quantise(0, 1)
         beta_quantise(1, 0)
         beta_norm_pass(1)
+        x_turn(0)
+        x_turn(1)
+        x_turn(2)
+        x_turn(3)
         beta_abs(2)
-        beta_norm_pass(2)
-        beta_abs(3)
-        beta_norm_pass(3)
         beta_regroup(2, 0, True)
         beta_regroup(2, 1, False)
         beta_quantise(1, 1)
+        x_quantise(0)
+        x_quantise(1)
         beta_quantise(2, 0)
-        beta_regroup(3, 1, False)
+        x_quantise(2)
+        x_quantise(3)
+        beta_norm_pass(2)
+        x_turn(4)
+        x_turn(5)
+        x_turn(6)
+        x_turn(7)
+        beta_abs(3)
         beta_regroup(3, 0, True)
+        beta_regroup(3, 1, False)
         beta_quantise(2, 1)
+        x_quantise(4)
+        x_quantise(5)
+        x_quantise(6)
+        x_quantise(7)
+        beta_norm_pass(3)
         norm_columns()
-
-        for i in range(2 * PASSES):
-            x_turn(i)
-        beta_quantise(3, 1)
         beta_quantise(3, 0)
-        for i in range(2 * PASSES):
-            x_quantise(i)
-
+        beta_quantise(3, 1)
         held["y_terms"] = big.tile([P, JT, B], F32, name="t_all", tag="raw_tt")
+        held["out_sb"] = big.tile([P, BT, N], F32, name="out_sb", tag="x_out")
         y_turn(0)
         y_turn(1)
-        for jt in range(4):
-            y_term(jt)
-        y_turn(2)
+        sum_on_vector(0, 0, NH, w2_sum[0])
         product(0)
-        y_turn(3)
-        for jt in range(4, JT):
-            y_term(jt)
+        y_term(0)
+        y_term(1)
+        y_turn(2)
+        y_term(2)
+        y_term(3)
         product(1)
+        y_turn(3)
+        sum_on_vector(1, 0, NH, w2_sum[1])
         product(2)
-
-        held["out_sb"] = big.tile([P, BT, N], F32, name="out_sb", tag="x_out")
-        sum_on_vector(w2[0][:], w2_sum[0][:])
-        sum_on_vector(w2[1][:], w2_sum[1][:])
-        sum_on_scalar(w2[3][:, left], half_a[3][:])
-        sum_on_scalar(w2[3][:, right], half_b[3][:])
+        y_term(4)
+        y_term(5)
+        y_term(6)
+        y_term(7)
+        sum_on_tensor(3)
+        sum_on_scalar(2, 0, 2048, part[2, 0])
         combine(0)
         product(3)
-        leave_psum(0)
         combine(1)
+        sum_on_vector(2, 2048, 4096, part[2, 1])
+        gather(3, nc.vector.tensor_copy)
+        total_on_tensor(3)
         product(4)
-        leave_psum(1)
-        store(0, 2)
-        sum_on_vector(w2[2][:], w2_sum[2][:])
-        sum_on_scalar(w2[6][:, left], half_a[6][:])
+        join_halves(2)
         combine(2)
         product(5)
-        join_halves(3)
+        leave_psum(0)
+        leave_psum(1)
+        store(0, 2)
+        sum_on_scalar(6, 0, 2048, part[6, 0])
+        sum_on_vector(4, 0, NH, w2_sum[4])
+        sum_on_tensor(5)
         combine(3)
         product(6)
+        gather(5, nc.vector.tensor_copy)
+        total_on_tensor(5)
         leave_psum(2)
         leave_psum(3)
         store(2, 4)
-        sum_on_scalar(w2[6][:, right], half_b[6][:])
-        sum_on_vector(w2[4][:], w2_sum[4][:])
         combine(4)
         product(7)
-        sum_on_vector(w2[5][:], w2_sum[5][:])
-        leave_psum(4)
-        sum_on_scalar(w2[7][:, left], half_a[7][:])
+        sum_on_vector(6, 2048, 4096, part[6, 1])
         combine(5)
-        join_halves(6)
-        combine(6)
+        sum_on_scalar(7, 0, 1536, part[7, 0])
+        leave_psum(4)
         leave_psum(5)
         store(4, 6)
+        join_halves(6)
+        combine(6)
         leave_psum(6)
         store(6, 7)
-        sum_on_vector(w2[7][:, right], half_b[7][:])
+        sum_on_vector(7, 1536, 4096, part[7, 1])
         join_halves(7)
-        combine(7)
-        leave_psum(7)
-        store(7, 8)
+        combine_halves(7)
+        leave_halves(7)
+        store_halves(7)

@@ -68,14 +68,11 @@ def tile_advresnet_kernel(tc, x, y, beta, bias_lin, W1, W2, bias1, bias2, adv, o
 
         raw = big.tile([P, PASSES * PASS_ELEMS], BF16, name="raw", tag="raw_tt")
         raw_planes = raw[:].rearrange("q (g t w) -> q g t w", g=PASSES, t=4)
-        for h in range(2):
-            for u in range(2):
-                nc.sync.dma_start(
-                    out=raw_planes[:, 0, 2 * u : 2 * u + 2, HALF * h : HALF * (h + 1)],
-                    in_=beta[0:K_PASS, HALF * h : HALF * (h + 1)].rearrange("(q t) w -> q t w", t=4)[
-                        :, 2 * u : 2 * u + 2, :
-                    ],
-                )
+        for u in range(2):
+            nc.sync.dma_start(
+                out=raw[:, 2 * N * u : 2 * N * (u + 1)],
+                in_=beta[0:K_PASS, :].rearrange("(q t) w -> q t w", t=4)[:, 2 * u : 2 * u + 2, :].rearrange("q t w -> q (t w)"),
+            )
         def load_beta(g):
             nc.sync.dma_start(
                 out=raw[:, PASS_ELEMS * g : PASS_ELEMS * (g + 1)],
@@ -106,13 +103,13 @@ def tile_advresnet_kernel(tc, x, y, beta, bias_lin, W1, W2, bias1, bias2, adv, o
         load_beta(2)
         load_x(1)
         load_beta(3)
-        load_w2(0, 0, NH)
         nc.sync.dma_start(out=y_sb[:], in_=y.rearrange("(p t) j -> p (t j)", t=BT))
+        load_w2(0, 0, NH)
         load_w2(1, 0, NH)
-        load_w2(3, 0, NH)
         load_w2(2, 0, NH)
-        load_w2(5, 0, NH)
+        load_w2(3, 0, NH)
         load_w2(4, 0, NH)
+        load_w2(5, 0, NH)
         load_w2(6, 0, NH)
         load_w2(7, 0,2048)
         load_w2(7, 2048,NH)
@@ -149,6 +146,17 @@ def tile_advresnet_kernel(tc, x, y, beta, bias_lin, W1, W2, bias1, bias2, adv, o
             )
             held["ab", g] = ab
 
+        def beta_abs_part(g, u):
+            if ("ab", g) not in held:
+                held["ab", g] = work.tile([P, PASS_ELEMS // 2], I32, name="ab", tag="ab")
+            half = PASS_ELEMS // 2
+            nc.vector.tensor_single_scalar(
+                out=held["ab", g][:, half // 2 * u : half // 2 * (u + 1)],
+                in_=raw[:, PASS_ELEMS * g + half * u : PASS_ELEMS * g + half * (u + 1)].bitcast(I32),
+                scalar=0x7FFF7FFF,
+                op=ALU.bitwise_and,
+            )
+
         def beta_regroup(g, h, on_vector):
             grouped = work.tile([P, 4 * HALF], BF16, name="gb", tag="gb", bufs=2 * PASSES, align_bytes=64)
             src = raw_planes[:, g, :, HALF * h : HALF * (h + 1)].rearrange("q t (c i) -> q c t i", i=4)
@@ -173,8 +181,11 @@ def tile_advresnet_kernel(tc, x, y, beta, bias_lin, W1, W2, bias1, bias2, adv, o
             )
 
         def beta_norm_pass(g):
+            beta_norm_part(g, 0, JT)
+
+        def beta_norm_part(g, first, end):
             planes = held["ab", g][:].bitcast(BF16)
-            for jt in range(JT):
+            for jt in range(first, end):
                 for t in range(4):
                     nc.tensor.matmul(
                         out=norm_ps[jt // 4][:, jt % 4, g, :],
@@ -350,98 +361,117 @@ def tile_advresnet_kernel(tc, x, y, beta, bias_lin, W1, W2, bias1, bias2, adv, o
             cols = slice(P * first, P * end)
             nc.sync.dma_start(out=out_rows[:, :, cols], in_=held["out_sb"][:, :, cols])
 
+        beta_abs_part(0, 0)
         beta_regroup(0, 0, True)
         beta_regroup(0, 1, False)
-        beta_abs(0)
-        beta_quantise(0, 0)
+        beta_abs_part(0, 1)
         bias_columns()
         beta_norm_pass(0)
         beta_abs(1)
         beta_regroup(1, 0, True)
         beta_regroup(1, 1, False)
-        beta_quantise(0, 1)
-        beta_quantise(1, 0)
+        beta_quantise(0, 0)
         beta_norm_pass(1)
         x_turn(0)
         x_turn(1)
         x_turn(2)
         x_turn(3)
-        beta_abs(2)
+        beta_quantise(0, 1)
         beta_regroup(2, 0, True)
+        beta_abs(2)
         beta_regroup(2, 1, False)
-        beta_quantise(1, 1)
-        x_quantise(0)
-        x_quantise(1)
-        beta_quantise(2, 0)
-        x_quantise(2)
-        x_quantise(3)
+        beta_quantise(1, 0)
         beta_norm_pass(2)
         x_turn(4)
         x_turn(5)
         x_turn(6)
         x_turn(7)
+        beta_quantise(1, 1)
+        x_quantise(0)
+        x_quantise(1)
         beta_abs(3)
+        beta_quantise(2, 0)
         beta_regroup(3, 0, True)
         beta_regroup(3, 1, False)
-        beta_quantise(2, 1)
+        x_quantise(2)
+        x_quantise(3)
+        beta_norm_pass(3)
         x_quantise(4)
         x_quantise(5)
         x_quantise(6)
         x_quantise(7)
-        beta_norm_pass(3)
         norm_columns()
+        beta_quantise(2, 1)
         beta_quantise(3, 0)
         beta_quantise(3, 1)
         held["y_terms"] = big.tile([P, JT, B], F32, name="t_all", tag="raw_tt")
         held["out_sb"] = big.tile([P, BT, N], F32, name="out_sb", tag="x_out")
         y_turn(0)
         y_turn(1)
+        product_pass(0, 0)
+        product_pass(1, 0)
+        product_pass(0, 1)
+        product_pass(1, 1)
+        product_pass(0, 2)
+        product_pass(1, 2)
+        product_pass(2, 0)
         sum_on_vector(0, 0, NH, w2_sum[0])
-        product(0)
         y_term(0)
         y_term(1)
         y_turn(2)
         y_term(2)
         y_term(3)
-        product(1)
         y_turn(3)
+        product_pass(0, 3)
+        product_pass(1, 3)
+        product_pass(2, 1)
+        product_pass(2, 2)
+        product_pass(2, 3)
         sum_on_vector(1, 0, NH, w2_sum[1])
-        product(2)
         y_term(4)
         y_term(5)
+        sum_on_tensor(3)
         y_term(6)
         y_term(7)
-        sum_on_tensor(3)
-        sum_on_scalar(2, 0, 2048, part[2, 0])
         combine(0)
-        product(3)
         combine(1)
+        sum_on_scalar(2, 0, 2048, part[2, 0])
         sum_on_vector(2, 2048, 4096, part[2, 1])
-        gather(3, nc.vector.tensor_copy)
-        total_on_tensor(3)
-        product(4)
-        join_halves(2)
-        combine(2)
-        product(5)
+        product_pass(3, 0)
+        product_pass(3, 1)
+        product_pass(3, 2)
+        product_pass(3, 3)
         leave_psum(0)
         leave_psum(1)
         store(0, 2)
-        sum_on_scalar(6, 0, 2048, part[6, 0])
-        sum_on_vector(4, 0, NH, w2_sum[4])
+        gather(3, nc.scalar.copy)
+        product_pass(4, 0)
+        product_pass(4, 1)
+        product_pass(4, 2)
+        product_pass(4, 3)
+        total_on_tensor(3)
         sum_on_tensor(5)
+        sum_on_vector(4, 0, NH, w2_sum[4])
+        join_halves(2)
+        combine(2)
+        product_pass(5, 0)
+        product_pass(5, 1)
+        product_pass(5, 2)
+        product_pass(5, 3)
+        sum_on_scalar(6, 0, 2048, part[6, 0])
         combine(3)
-        product(6)
+        combine(4)
         gather(5, nc.vector.tensor_copy)
         total_on_tensor(5)
+        product(6)
         leave_psum(2)
         leave_psum(3)
         store(2, 4)
-        combine(4)
         product(7)
+        leave_psum(4)
         sum_on_vector(6, 2048, 4096, part[6, 1])
         combine(5)
         sum_on_scalar(7, 0, 1536, part[7, 0])
-        leave_psum(4)
         leave_psum(5)
         store(4, 6)
         join_halves(6)

@@ -99,8 +99,8 @@ def tile_advresnet_kernel(tc, x, y, beta, bias_lin, W1, W2, bias1, bias2, adv, o
                 nc.sync.dma_start(out=w2[jt][:, first:end], in_=rows[:, first:end])
 
         load_beta(1)
-        load_x(0)
         load_beta(2)
+        load_x(0)
         load_x(1)
         load_beta(3)
         nc.sync.dma_start(out=y_sb[:], in_=y.rearrange("(p t) j -> p (t j)", t=BT))
@@ -128,12 +128,14 @@ def tile_advresnet_kernel(tc, x, y, beta, bias_lin, W1, W2, bias1, bias2, adv, o
         out_rows = out.rearrange("(p t) j -> p t j", t=BT)
         held = {}
 
-        bias_t = ps_c.tile([P, P], BF16, name="bt_ps", tag="c")
-        nc.tensor.transpose(out=bias_t[:], in_=brows[:], identity=ident_b[:])
-        norm_ps = [ps_b.tile([P, JT // 2, PASSES, ONES_N], F32, name="bn_%d" % i, tag="b") for i in range(2)]
+        norm_ps = ps_b.tile([P, JT, PASSES, ONES_N], F32, name="norm_ps", tag="b")
+
+        def bias_turn():
+            held["bias_t"] = ps_c.tile([P, P], BF16, name="bt_ps", tag="c")
+            nc.tensor.transpose(out=held["bias_t"][:], in_=brows[:], identity=ident_b[:])
 
         def bias_columns():
-            nc.vector.tensor_copy(out=b16[:], in_=bias_t[:, 0 : 2 * JT])
+            nc.vector.tensor_copy(out=b16[:], in_=held["bias_t"][:, 0 : 2 * JT])
             nc.vector.tensor_tensor(out=bsum[:], in0=b16[:, 0:JT], in1=b16[:, JT : 2 * JT], op=ALU.add)
 
         def beta_abs(g):
@@ -188,7 +190,7 @@ def tile_advresnet_kernel(tc, x, y, beta, bias_lin, W1, W2, bias1, bias2, adv, o
             for jt in range(first, end):
                 for t in range(4):
                     nc.tensor.matmul(
-                        out=norm_ps[jt // 4][:, jt % 4, g, :],
+                        out=norm_ps[:, jt, g, :],
                         lhsT=planes[:, N * t + P * jt : N * t + P * (jt + 1)],
                         rhs=ones[:],
                         start=(t == 0),
@@ -196,15 +198,15 @@ def tile_advresnet_kernel(tc, x, y, beta, bias_lin, W1, W2, bias1, bias2, adv, o
                     )
 
         def norm_columns():
-            for i in range(2):
-                nc.vector.tensor_reduce(
-                    out=norm[:, 4 * i : 4 * (i + 1)], in_=norm_ps[i][:, :, :, 0], axis=mybir.AxisListType.X, op=ALU.add
-                )
+            nc.vector.tensor_reduce(
+                out=norm[:], in_=norm_ps[:, :, :, 0], axis=mybir.AxisListType.X, op=ALU.add
+            )
             nc.vector.tensor_scalar_mul(out=y_scale[:], in0=norm[:], scalar1=-EPSILON)
 
         def x_turn(i):
             h, g = i // PASSES, i % PASSES
-            turned = ps_a.tile([P, 2, 2 * P], F32, name="xt", tag="a")
+            pool, tag = (ps_c, "c") if g == PASSES - 1 else (ps_a, "a")
+            turned = pool.tile([P, 2, 2 * P], F32, name="xt", tag=tag)
             for u in range(2):
                 for s in range(2):
                     w0 = (K // 2) * (2 * h + s) + 256 * g
@@ -365,41 +367,43 @@ def tile_advresnet_kernel(tc, x, y, beta, bias_lin, W1, W2, bias1, bias2, adv, o
         beta_regroup(0, 0, True)
         beta_regroup(0, 1, False)
         beta_abs_part(0, 1)
-        bias_columns()
         beta_norm_pass(0)
         beta_abs(1)
-        beta_regroup(1, 0, True)
+        beta_regroup_part(1, 0, 0, 384, nc.vector.tensor_copy)
         beta_regroup(1, 1, False)
+        beta_regroup_part(1, 0, 384, 512, nc.scalar.copy)
         beta_quantise(0, 0)
         beta_norm_pass(1)
+        beta_regroup(2, 0, True)
+        beta_quantise(0, 1)
+        beta_abs(2)
+        beta_regroup(2, 1, False)
+        beta_quantise(1, 0)
         x_turn(0)
         x_turn(1)
         x_turn(2)
         x_turn(3)
-        beta_quantise(0, 1)
-        beta_regroup(2, 0, True)
-        beta_abs(2)
-        beta_regroup(2, 1, False)
-        beta_quantise(1, 0)
-        beta_norm_pass(2)
         x_turn(4)
         x_turn(5)
         x_turn(6)
         x_turn(7)
+        beta_norm_pass(2)
+        bias_turn()
         beta_quantise(1, 1)
+        beta_quantise(2, 0)
         x_quantise(0)
         x_quantise(1)
-        beta_abs(3)
-        beta_quantise(2, 0)
-        beta_regroup(3, 0, True)
-        beta_regroup(3, 1, False)
         x_quantise(2)
         x_quantise(3)
+        beta_abs(3)
+        beta_regroup(3, 0, True)
+        beta_regroup(3, 1, False)
         beta_norm_pass(3)
         x_quantise(4)
         x_quantise(5)
         x_quantise(6)
         x_quantise(7)
+        bias_columns()
         norm_columns()
         beta_quantise(2, 1)
         beta_quantise(3, 0)
@@ -411,17 +415,17 @@ def tile_advresnet_kernel(tc, x, y, beta, bias_lin, W1, W2, bias1, bias2, adv, o
         product_pass(0, 0)
         product_pass(1, 0)
         product_pass(0, 1)
-        product_pass(1, 1)
-        product_pass(0, 2)
-        product_pass(1, 2)
-        product_pass(2, 0)
-        sum_on_vector(0, 0, NH, w2_sum[0])
         y_term(0)
         y_term(1)
         y_turn(2)
+        product_pass(1, 1)
+        sum_on_vector(0, 0, NH, w2_sum[0])
         y_term(2)
         y_term(3)
+        product_pass(0, 2)
+        product_pass(1, 2)
         y_turn(3)
+        product_pass(2, 0)
         product_pass(0, 3)
         product_pass(1, 3)
         product_pass(2, 1)
@@ -451,18 +455,18 @@ def tile_advresnet_kernel(tc, x, y, beta, bias_lin, W1, W2, bias1, bias2, adv, o
         product_pass(4, 3)
         total_on_tensor(3)
         sum_on_tensor(5)
-        sum_on_vector(4, 0, NH, w2_sum[4])
         join_halves(2)
         combine(2)
+        sum_on_vector(4, 0, NH, w2_sum[4])
         product_pass(5, 0)
         product_pass(5, 1)
         product_pass(5, 2)
         product_pass(5, 3)
         sum_on_scalar(6, 0, 2048, part[6, 0])
         combine(3)
-        combine(4)
         gather(5, nc.vector.tensor_copy)
         total_on_tensor(5)
+        combine(4)
         product(6)
         leave_psum(2)
         leave_psum(3)
@@ -474,11 +478,11 @@ def tile_advresnet_kernel(tc, x, y, beta, bias_lin, W1, W2, bias1, bias2, adv, o
         sum_on_scalar(7, 0, 1536, part[7, 0])
         leave_psum(5)
         store(4, 6)
+        sum_on_vector(7, 1536, 4096, part[7, 1])
         join_halves(6)
         combine(6)
         leave_psum(6)
         store(6, 7)
-        sum_on_vector(7, 1536, 4096, part[7, 1])
         join_halves(7)
         combine_halves(7)
         leave_halves(7)

@@ -28,7 +28,7 @@ FLOPS = 2 * B * K * N
 BYTES = 2 * (B * K + B * N + K * N + N * NH + 2 * N) + 4 * B * N
 
 PE_TILES = (3, 5,)
-SPLIT_TILES = (2, 6, 7,)
+SPLIT_TILES = (2, 4, 6, 7,)
 SPREAD = 4
 PE_COLS = NH // SPREAD
 PE_ROWS = P // SPREAD
@@ -112,7 +112,8 @@ def tile_advresnet_kernel(tc, x, y, beta, bias_lin, W1, W2, bias1, bias2, adv, o
         load_w2(5, 0, NH)
         load_w2(6, 0, NH)
         load_w2(7, 0,2048)
-        load_w2(7, 2048,NH)
+        load_w2(7, 2048,3072)
+        load_w2(7, 3072,NH)
 
         codes_b = big.tile([P, PASSES * N], U32, name="codes_b", align_bytes=64)
         scales_b = big.tile([P, PASSES * N], U8, name="plane_b", align_bytes=64)
@@ -123,7 +124,7 @@ def tile_advresnet_kernel(tc, x, y, beta, bias_lin, W1, W2, bias1, bias2, adv, o
         norm = const.tile([P, JT], F32, name="sraw")
         y_scale = const.tile([P, JT], F32, name="s_col")
         w2_sum = dict((jt, const.tile([P, 1], F32, name="c_%d" % jt)) for jt in range(JT) if jt not in PE_TILES)
-        part = dict(((jt, i), const.tile([P, 1], F32, name="part_%d_%d" % (jt, i))) for jt in SPLIT_TILES for i in range(2))
+        part = dict(((jt, i), const.tile([P, 1], F32, name="part_%d_%d" % (jt, i))) for jt in SPLIT_TILES for i in range(4))
         x_words = x_sb[:].bitcast(F32)
         out_rows = out.rearrange("(p t) j -> p t j", t=BT)
         held = {}
@@ -441,49 +442,43 @@ def tile_advresnet_kernel(tc, x, y, beta, bias_lin, W1, W2, bias1, bias2, adv, o
         combine(1)
         sum_on_scalar(2, 0, 2048, part[2, 0])
         sum_on_vector(2, 2048, 4096, part[2, 1])
-        product_pass(3, 0)
-        product_pass(3, 1)
-        product_pass(3, 2)
-        product_pass(3, 3)
+        product(3)
         leave_psum(0)
         leave_psum(1)
         store(0, 2)
         gather(3, nc.scalar.copy)
-        product_pass(4, 0)
-        product_pass(4, 1)
-        product_pass(4, 2)
-        product_pass(4, 3)
+        product(4)
         total_on_tensor(3)
         sum_on_tensor(5)
         join_halves(2)
         combine(2)
-        sum_on_vector(4, 0, NH, w2_sum[4])
-        product_pass(5, 0)
-        product_pass(5, 1)
-        product_pass(5, 2)
-        product_pass(5, 3)
-        sum_on_scalar(6, 0, 2048, part[6, 0])
+        sum_on_scalar(4, 0, 2048, part[4, 0])
+        sum_on_vector(4, 2048, 4096, part[4, 1])
+        product(5)
         combine(3)
         gather(5, nc.vector.tensor_copy)
         total_on_tensor(5)
+        join_halves(4)
         combine(4)
         product(6)
         leave_psum(2)
+        sum_on_scalar(6, 0, 1536, part[6, 0])
+        product(7)
+        sum_on_vector(6, 1536, 4096, part[6, 1])
+        combine(5)
         leave_psum(3)
         store(2, 4)
-        product(7)
+        sum_on_scalar(7, 0, 1024, part[7, 0])
         leave_psum(4)
-        sum_on_vector(6, 2048, 4096, part[6, 1])
-        combine(5)
-        sum_on_scalar(7, 0, 1536, part[7, 0])
         leave_psum(5)
         store(4, 6)
-        sum_on_vector(7, 1536, 4096, part[7, 1])
         join_halves(6)
+        sum_on_vector(7, 1024, 3072, part[7, 2])
         combine(6)
+        nc.vector.tensor_tensor(out=part[7, 3][:], in0=part[7, 0][:], in1=part[7, 2][:], op=ALU.add)
+        sum_on_vector(7, 3072, 4096, w2_sum[7], before=part[7, 3])
         leave_psum(6)
         store(6, 7)
-        join_halves(7)
         combine_halves(7)
         leave_halves(7)
         store_halves(7)

from contextlib import ExitStack

import concourse.mybir as mybir
from concourse.masks import make_identity

F32 = mybir.dt.float32
BF16 = mybir.dt.bfloat16
I32 = mybir.dt.int32
U32 = mybir.dt.uint32
U8 = mybir.dt.uint8
FP8X4 = mybir.dt.float8_e4m3fn_x4
ALU = mybir.AluOpType
ACT = mybir.ActivationFunctionType

P = 128
B, K, NH, N = 512, 2048, 4096, 1024
EPSILON = 0.1
K_PASS = 4 * P
PASSES = K // K_PASS
PASS_ELEMS = 4 * N
HALF = N // 2
JT = N // P
BT = B // P
W2_HALF = NH // 2
ONES_N = 16

FLOPS = 2 * B * K * N
BYTES = 2 * (B * K + B * N + K * N + N * NH + 2 * N) + 4 * B * N

PE_TILES = (3, 5,)
SPLIT_TILES = (2, 4, 6, 7,)
SPREAD = 4
PE_COLS = NH // SPREAD
PE_ROWS = P // SPREAD


def tile_advresnet_kernel(tc, x, y, beta, bias_lin, W1, W2, bias1, bias2, adv, out):
    assert adv == 1
    nc = tc.nc
    with ExitStack() as ctx:
        const = ctx.enter_context(tc.tile_pool(name="const", bufs=1))
        big = ctx.enter_context(tc.tile_pool(name="big", bufs=1))
        work = ctx.enter_context(tc.tile_pool(name="work", bufs=2))
        ps_a = ctx.enter_context(tc.psum_pool(name="ps_a", bufs=3))
        ps_b = ctx.enter_context(tc.psum_pool(name="ps_b", bufs=3))
        ps_c = ctx.enter_context(tc.psum_pool(name="ps_c", bufs=2))
        ctx.enter_context(tc.manual_schedule())

        brows = const.tile([P, P], BF16, name="brows")
        nc.gpsimd.memset(brows[:], 0.0)
        ones = const.tile([P, ONES_N], BF16, name="ones")
        nc.vector.memset(ones[:], 1.0)
        table_load = const.tile([P, 1], BF16, name="table_load")
        nc.scalar.copy(out=table_load[:], in_=ones[:, 0:1])
        nc.scalar.dma_start(out=brows[0:JT, :], in_=bias_lin.rearrange("(r c) -> r c", c=P))
        nc.scalar.dma_start(out=brows[JT : 2 * JT, :], in_=bias2.rearrange("(r c) -> r c", c=P))
        ident_b = const.tile([P, P], BF16, name="ident_b")
        make_identity(nc, ident_b[:])
        ident_f = const.tile([P, P], F32, name="ident_f")
        make_identity(nc, ident_f[:])

        pairs = const.tile([P, P // 2], BF16, name="pairs")
        nc.vector.tensor_tensor(out=pairs[:], in0=ident_b[:, 0::2], in1=ident_b[:, 1::2], op=ALU.add)
        quads = const.tile([P, PE_ROWS], BF16, name="quads")
        nc.vector.tensor_tensor(out=quads[:], in0=pairs[:, 0::2], in1=pairs[:, 1::2], op=ALU.add)
        factor = const.tile([P, 1], F32, name="factor")
        nc.vector.memset(factor[:], float(NH))

        raw = big.tile([P, PASSES * PASS_ELEMS], BF16, name="raw", tag="raw_tt")
        raw_planes = raw[:].rearrange("q (g t w) -> q g t w", g=PASSES, t=4)
        for u in range(2):
            nc.sync.dma_start(
                out=raw[:, 2 * N * u : 2 * N * (u + 1)],
                in_=beta[0:K_PASS, :].rearrange("(q t) w -> q t w", t=4)[:, 2 * u : 2 * u + 2, :].rearrange("q t w -> q (t w)"),
            )
        def load_beta(g):
            nc.sync.dma_start(
                out=raw[:, PASS_ELEMS * g : PASS_ELEMS * (g + 1)],
                in_=beta[K_PASS * g : K_PASS * (g + 1), :].rearrange("(q t) w -> q (t w)", t=4),
            )

        x_sb = big.tile([P, BT * K], BF16, name="x_sb", tag="x_out")
        x_rows = x.rearrange("(p t) k -> p (t k)", t=BT)

        def load_x(h):
            nc.sync.dma_start(out=x_sb[:, 2 * K * h : 2 * K * (h + 1)], in_=x_rows[:, 2 * K * h : 2 * K * (h + 1)])

        y_sb = big.tile([P, BT * N], BF16, name="y_sb")
        w2 = [big.tile([P, NH], BF16, name="w2_%d" % jt) for jt in range(JT)]

        def load_w2(jt, first, end):
            rows = W2[P * jt : P * (jt + 1), :]
            if jt in PE_TILES:
                nc.sync.dma_start(
                    out=w2[jt][:].rearrange("p (s w) -> p s w", s=SPREAD),
                    in_=rows.rearrange("(s r) (c w) -> (r c) s w", s=SPREAD, c=SPREAD),
                )
            else:
                nc.sync.dma_start(out=w2[jt][:, first:end], in_=rows[:, first:end])

        load_beta(1)
        load_beta(2)
        load_x(0)
        load_x(1)
        load_beta(3)
        nc.sync.dma_start(out=y_sb[:], in_=y.rearrange("(p t) j -> p (t j)", t=BT))
        load_w2(0, 0, NH)
        load_w2(1, 0, NH)
        load_w2(2, 0, NH)
        load_w2(3, 0, NH)
        load_w2(4, 0, NH)
        load_w2(5, 0, NH)
        load_w2(6, 0, NH)
        load_w2(7, 0,2048)
        load_w2(7, 2048,3072)
        load_w2(7, 3072,NH)

        codes_b = big.tile([P, PASSES * N], U32, name="codes_b", align_bytes=64)
        scales_b = big.tile([P, PASSES * N], U8, name="plane_b", align_bytes=64)
        codes_x = big.tile([P, PASSES * B], U32, name="codes_x", align_bytes=64)
        scales_x = big.tile([P, PASSES * B], U8, name="plane_x", align_bytes=64)
        b16 = const.tile([P, 2 * JT], F32, name="b16")
        bsum = const.tile([P, JT], F32, name="bsum")
        norm = const.tile([P, JT], F32, name="sraw")
        y_scale = const.tile([P, JT], F32, name="s_col")
        w2_sum = dict((jt, const.tile([P, 1], F32, name="c_%d" % jt)) for jt in range(JT) if jt not in PE_TILES)
        part = dict(((jt, i), const.tile([P, 1], F32, name="part_%d_%d" % (jt, i))) for jt in SPLIT_TILES for i in range(4))
        x_words = x_sb[:].bitcast(F32)
        out_rows = out.rearrange("(p t) j -> p t j", t=BT)
        held = {}

        norm_ps = ps_b.tile([P, JT, PASSES, ONES_N], F32, name="norm_ps", tag="b")

        def bias_turn():
            held["bias_t"] = ps_c.tile([P, P], BF16, name="bt_ps", tag="c")
            nc.tensor.transpose(out=held["bias_t"][:], in_=brows[:], identity=ident_b[:])

        def bias_columns():
            nc.vector.tensor_copy(out=b16[:], in_=held["bias_t"][:, 0 : 2 * JT])
            nc.vector.tensor_tensor(out=bsum[:], in0=b16[:, 0:JT], in1=b16[:, JT : 2 * JT], op=ALU.add)

        def beta_abs(g):
            ab = work.tile([P, PASS_ELEMS // 2], I32, name="ab", tag="ab")
            nc.vector.tensor_single_scalar(
                out=ab[:],
                in_=raw[:, PASS_ELEMS * g : PASS_ELEMS * (g + 1)].bitcast(I32),
                scalar=0x7FFF7FFF,
                op=ALU.bitwise_and,
            )
            held["ab", g] = ab

        def beta_abs_part(g, u):
            if ("ab", g) not in held:
                held["ab", g] = work.tile([P, PASS_ELEMS // 2], I32, name="ab", tag="ab")
            half = PASS_ELEMS // 2
            nc.vector.tensor_single_scalar(
                out=held["ab", g][:, half // 2 * u : half // 2 * (u + 1)],
                in_=raw[:, PASS_ELEMS * g + half * u : PASS_ELEMS * g + half * (u + 1)].bitcast(I32),
                scalar=0x7FFF7FFF,
                op=ALU.bitwise_and,
            )

        def beta_regroup(g, h, on_vector):
            grouped = work.tile([P, 4 * HALF], BF16, name="gb", tag="gb", bufs=2 * PASSES, align_bytes=64)
            src = raw_planes[:, g, :, HALF * h : HALF * (h + 1)].rearrange("q t (c i) -> q c t i", i=4)
            dst = grouped[:].rearrange("q (c i t) -> q c t i", i=4, t=4)
            if on_vector:
                nc.vector.tensor_copy(out=dst, in_=src)
            else:
                nc.scalar.copy(out=dst, in_=src)
            held["gb", g, h] = grouped

        def beta_regroup_part(g, h, first, end, copy):
            if ("gb", g, h) not in held:
                held["gb", g, h] = work.tile([P, 4 * HALF], BF16, name="gb", tag="gb", bufs=2 * PASSES, align_bytes=64)
            src = raw_planes[:, g, :, HALF * h + first : HALF * h + end].rearrange("q t (c i) -> q c t i", i=4)
            dst = held["gb", g, h][:, 4 * first : 4 * end].rearrange("q (c i t) -> q c t i", i=4, t=4)
            copy(out=dst, in_=src)

        def beta_quantise(g, h):
            cols = slice(N * g + HALF * h, N * g + HALF * (h + 1))
            nc.vector.quantize_mx(
                out=codes_b[:, cols].bitcast(FP8X4), scales=scales_b[:, cols], in_=held["gb", g, h][:]
            )

        def beta_norm_pass(g):
            beta_norm_part(g, 0, JT)

        def beta_norm_part(g, first, end):
            planes = held["ab", g][:].bitcast(BF16)
            for jt in range(first, end):
                for t in range(4):
                    nc.tensor.matmul(
                        out=norm_ps[:, jt, g, :],
                        lhsT=planes[:, N * t + P * jt : N * t + P * (jt + 1)],
                        rhs=ones[:],
                        start=(t == 0),
                        stop=(t == 3),
                    )

        def norm_columns():
            nc.vector.tensor_reduce(
                out=norm[:], in_=norm_ps[:, :, :, 0], axis=mybir.AxisListType.X, op=ALU.add
            )
            nc.vector.tensor_scalar_mul(out=y_scale[:], in0=norm[:], scalar1=-EPSILON)

        def x_turn(i):
            h, g = i // PASSES, i % PASSES
            pool, tag = (ps_c, "c") if g == PASSES - 1 else (ps_a, "a")
            turned = pool.tile([P, 2, 2 * P], F32, name="xt", tag=tag)
            for u in range(2):
                for s in range(2):
                    w0 = (K // 2) * (2 * h + s) + 256 * g
                    nc.tensor.transpose(
                        out=turned[:, u, P * s : P * (s + 1)],
                        in_=x_words[:, w0 + u : w0 + 256 : 2],
                        identity=ident_f[:],
                    )
            grouped = work.tile([P, 8 * P], BF16, name="gx", tag="gx", bufs=2 * PASSES, align_bytes=64)
            nc.scalar.copy(
                out=grouped[:].bitcast(F32).rearrange("q (c u) -> q c u", u=2),
                in_=turned[:].rearrange("q u c -> q c u"),
            )
            held["gx", i] = grouped

        def x_quantise(i):
            h, g = i // PASSES, i % PASSES
            cols = slice(B * g + 2 * P * h, B * g + 2 * P * (h + 1))
            nc.vector.quantize_mx(out=codes_x[:, cols].bitcast(FP8X4), scales=scales_x[:, cols], in_=held["gx", i][:])

        def y_turn(m):
            turned = ps_c.tile([P, 2, B], BF16, name="y_t", tag="c")
            for i in range(2):
                jt = 2 * m + i
                for t in range(BT):
                    nc.tensor.transpose(
                        out=turned[:, i, P * t : P * (t + 1)],
                        in_=y_sb[:, N * t + P * jt : N * t + P * (jt + 1)],
                        identity=ident_b[:],
                    )
            held["y_t", m] = turned

        def y_term(jt):
            nc.scalar.activation(
                out=held["y_terms"][:, jt, :],
                in_=held["y_t", jt // 2][:, jt % 2, :],
                func=ACT.Identity,
                scale=y_scale[:, jt : jt + 1],
                bias=bsum[:, jt : jt + 1],
            )

        def product_pass(jt, g):
            if g == 0:
                held["mm", jt] = ps_a.tile([P, B], F32, name="mm", tag="a")
            j_cols = slice(N * g + P * jt, N * g + P * (jt + 1))
            b_cols = slice(B * g, B * (g + 1))
            nc.tensor.matmul_mx(
                out=held["mm", jt][:],
                lhsT=codes_b[:, j_cols].bitcast(FP8X4),
                lhsT_scale=scales_b[:, j_cols],
                rhs=codes_x[:, b_cols].bitcast(FP8X4),
                rhs_scale=scales_x[:, b_cols],
                start=(g == 0),
                stop=(g == PASSES - 1),
            )

        def product(jt):
            for g in range(PASSES):
                product_pass(jt, g)

        def sum_on_vector(jt, first, end, total, before=None):
            piece = w2[jt][:, first:end]
            nc.vector.tensor_scalar(
                out=piece,
                in0=piece,
                scalar1=float(NH),
                scalar2=None if before is None else before[:],
                op0=ALU.mult,
                op1=ALU.add,
                accum_out=total[:],
            )

        def sum_on_scalar(jt, first, end, total):
            piece = w2[jt][:, first:end]
            nc.scalar.activation(out=piece, in_=piece, func=ACT.Copy, scale=float(NH), accum_out=total[:])

        def join_halves(jt):
            nc.vector.tensor_tensor(out=w2_sum[jt][:], in0=part[jt, 0][:], in1=part[jt, 1][:], op=ALU.add)

        def sum_on_tensor(jt):
            sums = ps_c.tile([P, P + 1], F32, name="w2_ps", tag="c")
            for s in range(SPREAD):
                for i in range(PE_COLS // P):
                    c0 = PE_COLS * s + P * i
                    nc.tensor.matmul(
                        out=sums[:, PE_ROWS * s : PE_ROWS * (s + 1)],
                        lhsT=w2[jt][:, c0 : c0 + P],
                        rhs=quads[:],
                        start=(i == 0),
                        stop=(i == PE_COLS // P - 1),
                    )
            held["w2_ps", jt] = sums

        def gather(jt, copy):
            held["partial", jt] = work.tile([P, P], F32, name="partial", tag="partial")
            copy(out=held["partial", jt][:], in_=held["w2_ps", jt][:, 0:P])

        def total_on_tensor(jt):
            held["total", jt] = held["w2_ps", jt][:, P : P + 1]
            nc.tensor.matmul(
                out=held["total", jt], lhsT=held["partial", jt][:], rhs=factor[:], start=True, stop=True
            )

        def combine(jt):
            tile_t = work.tile([P, B], F32, name="o_t", tag="o_t", bufs=3)
            nc.vector.scalar_tensor_tensor(
                out=tile_t[:],
                in0=held["mm", jt][:],
                scalar=held["total", jt] if jt in PE_TILES else w2_sum[jt][:],
                in1=held["y_terms"][:, jt, :],
                op0=ALU.add,
                op1=ALU.add,
            )
            turned = ps_b.tile([P, BT, P], F32, name="o_ps", tag="b")
            for t in range(BT):
                nc.tensor.transpose(out=turned[:, t, :], in_=tile_t[:, P * t : P * (t + 1)], identity=ident_f[:])
            held["o_ps", jt] = turned

        def combine_halves(jt):
            tile_t = work.tile([P, B], F32, name="o_t", tag="o_t", bufs=3)
            turned = [ps_b.tile([P, 2, P], F32, name="o_half%d" % i, tag="b") for i in range(2)]
            held["o_half", jt] = turned
            for i in range(2):
                cols = slice(B // 2 * i, B // 2 * (i + 1))
                nc.vector.scalar_tensor_tensor(
                    out=tile_t[:, cols],
                    in0=held["mm", jt][:, cols],
                    scalar=held["total", jt] if jt in PE_TILES else w2_sum[jt][:],
                    in1=held["y_terms"][:, jt, cols],
                    op0=ALU.add,
                    op1=ALU.add,
                )
            for i in range(2):
                for t in range(2):
                    nc.tensor.transpose(
                        out=turned[i][:, t, :], in_=tile_t[:, P * (2 * i + t) : P * (2 * i + t + 1)], identity=ident_f[:]
                    )

        def leave_halves(jt):
            nc.scalar.copy(out=held["out_sb"][:, 0:2, P * jt : P * (jt + 1)], in_=held["o_half", jt][0][:])
            nc.vector.tensor_copy(out=held["out_sb"][:, 2:4, P * jt : P * (jt + 1)], in_=held["o_half", jt][1][:])

        def store_halves(jt):
            cols = slice(P * jt, P * (jt + 1))
            for i in range(2):
                nc.sync.dma_start(
                    out=out_rows[:, 2 * i : 2 * (i + 1), cols], in_=held["out_sb"][:, 2 * i : 2 * (i + 1), cols]
                )

        def leave_psum(jt):
            nc.scalar.copy(out=held["out_sb"][:, :, P * jt : P * (jt + 1)], in_=held["o_ps", jt][:])

        def store(first, end):
            cols = slice(P * first, P * end)
            nc.sync.dma_start(out=out_rows[:, :, cols], in_=held["out_sb"][:, :, cols])

        beta_abs_part(0, 0)
        beta_regroup(0, 0, True)
        beta_regroup(0, 1, False)
        beta_abs_part(0, 1)
        beta_norm_pass(0)
        beta_abs(1)
        beta_regroup_part(1, 0, 0, 384, nc.vector.tensor_copy)
        beta_regroup(1, 1, False)
        beta_regroup_part(1, 0, 384, 512, nc.scalar.copy)
        beta_quantise(0, 0)
        beta_norm_pass(1)
        beta_regroup(2, 0, True)
        beta_quantise(0, 1)
        beta_abs(2)
        beta_regroup(2, 1, False)
        beta_quantise(1, 0)
        x_turn(0)
        x_turn(1)
        x_turn(2)
        x_turn(3)
        x_turn(4)
        x_turn(5)
        x_turn(6)
        x_turn(7)
        beta_norm_pass(2)
        bias_turn()
        beta_quantise(1, 1)
        beta_quantise(2, 0)
        x_quantise(0)
        x_quantise(1)
        x_quantise(2)
        x_quantise(3)
        beta_abs(3)
        beta_regroup(3, 0, True)
        beta_regroup(3, 1, False)
        beta_norm_pass(3)
        x_quantise(4)
        x_quantise(5)
        x_quantise(6)
        x_quantise(7)
        bias_columns()
        norm_columns()
        beta_quantise(2, 1)
        beta_quantise(3, 0)
        beta_quantise(3, 1)
        held["y_terms"] = big.tile([P, JT, B], F32, name="t_all", tag="raw_tt")
        held["out_sb"] = big.tile([P, BT, N], F32, name="out_sb", tag="x_out")
        y_turn(0)
        y_turn(1)
        product_pass(0, 0)
        product_pass(1, 0)
        product_pass(0, 1)
        y_term(0)
        y_term(1)
        y_turn(2)
        product_pass(1, 1)
        sum_on_vector(0, 0, NH, w2_sum[0])
        y_term(2)
        y_term(3)
        product_pass(0, 2)
        product_pass(1, 2)
        y_turn(3)
        product_pass(2, 0)
        product_pass(0, 3)
        product_pass(1, 3)
        product_pass(2, 1)
        product_pass(2, 2)
        product_pass(2, 3)
        sum_on_vector(1, 0, NH, w2_sum[1])
        y_term(4)
        y_term(5)
        sum_on_tensor(3)
        y_term(6)
        y_term(7)
        combine(0)
        combine(1)
        sum_on_scalar(2, 0, 2048, part[2, 0])
        sum_on_vector(2, 2048, 4096, part[2, 1])
        product(3)
        leave_psum(0)
        leave_psum(1)
        store(0, 2)
        gather(3, nc.scalar.copy)
        product(4)
        total_on_tensor(3)
        sum_on_tensor(5)
        join_halves(2)
        combine(2)
        sum_on_scalar(4, 0, 2048, part[4, 0])
        sum_on_vector(4, 2048, 4096, part[4, 1])
        product(5)
        combine(3)
        gather(5, nc.vector.tensor_copy)
        total_on_tensor(5)
        join_halves(4)
        combine(4)
        product(6)
        leave_psum(2)
        sum_on_scalar(6, 0, 1536, part[6, 0])
        product(7)
        sum_on_vector(6, 1536, 4096, part[6, 1])
        combine(5)
        leave_psum(3)
        store(2, 4)
        sum_on_scalar(7, 0, 1024, part[7, 0])
        leave_psum(4)
        leave_psum(5)
        store(4, 6)
        join_halves(6)
        sum_on_vector(7, 1024, 3072, part[7, 2])
        combine(6)
        nc.vector.tensor_tensor(out=part[7, 3][:], in0=part[7, 0][:], in1=part[7, 2][:], op=ALU.add)
        sum_on_vector(7, 3072, 4096, w2_sum[7], before=part[7, 3])
        leave_psum(6)
        store(6, 7)
        combine_halves(7)
        leave_halves(7)
        store_halves(7)
